import numpy as np
import ml_dtypes

BF16 = ml_dtypes.bfloat16


def bf(x):
    return np.asarray(x, np.float32).astype(BF16)


def f32(x):
    return np.asarray(x, np.float32)


def f64(x):
    return np.asarray(x).astype(np.float64)


def striped(idx):
    return np.tile(idx.reshape(-1, 16).T, (8, 1))


S, D, Q, M, N = 256, 128, 384, 512, 128


def setup_inputs():
    return {"table": bf(np.random.standard_normal((S, D))), "pos": bf(0.5 * np.random.standard_normal((D, N))), "w": bf(np.random.standard_normal((D, Q)) / np.sqrt(D)), "b": f32(0.1 * np.random.standard_normal((Q, 1))), "offs": striped(np.random.permutation(np.tile(np.arange(S), 2))[:N])}


def reference(table, pos, w, b, offs):
    idx = offs[:16].T.reshape(-1)
    y = f64(table)[idx].T + f64(pos)
    return np.concatenate([f64(w).T @ y + f64(b), y], axis=0)

@@ -1,0 +1,57 @@
+import concourse.mybir as mybir
+from concourse.masks import make_identity
+
+BF16, F32, U16 = mybir.dt.bfloat16, mybir.dt.float32, mybir.dt.uint16
+
+P = 128
+WORDS = 256
+TOKENS = 128
+Q = 384
+Q_BLOCKS = Q // P
+WORD_BLOCKS = WORDS // P
+
+FLOPS = 2 * P * Q * TOKENS
+
+
+def tile_transformertranducer_kernel(tc, table, pos, w, b, offs, out):
+    nc = tc.nc
+    with (
+        tc.tile_pool(name="held", bufs=1) as held,
+        tc.psum_pool(name="psum", bufs=1) as psum,
+    ):
+        word_rows = [held.tile([P, P], BF16, name=f"word_rows{h}") for h in range(WORD_BLOCKS)]
+        nc.sync.dma_start(word_rows[0][:], table[0:P, :])
+        nc.scalar.dma_start(word_rows[1][:], table[P : 2 * P, :])
+        offsets = held.tile([P, TOKENS // 16], U16, name="offsets")
+        nc.sync.dma_start(offsets[:], offs)
+        weights = held.tile([P, Q], BF16, name="weights")
+        nc.scalar.dma_start(weights[:], w)
+        positions = held.tile([P, TOKENS], BF16, name="positions")
+        nc.sync.dma_start(positions[:], pos)
+        bias = held.tile([P, Q_BLOCKS], F32, name="bias")
+        with nc.allow_non_contiguous_dma(reason="384 bias values, one to a partition and block"):
+            nc.scalar.dma_start(bias[:], b.rearrange("(c p) one -> p (c one)", p=P))
+
+        identity = held.tile([P, P], BF16, name="identity")
+        make_identity(nc, identity[:])
+
+        window = held.tile([P, WORDS], BF16, name="window")
+        for h in range(WORD_BLOCKS):
+            flipped = psum.tile([P, P], BF16, name=f"flipped{h}")
+            nc.tensor.transpose(flipped[:], word_rows[h][:], identity[:])
+            nc.vector.tensor_copy(window[:, h * P : (h + 1) * P], flipped[:])
+
+        stationary = [weights[:, c * P : (c + 1) * P] for c in range(Q_BLOCKS)] + [identity[:]]
+        sums = [psum.tile([P, TOKENS], F32, name=f"sums{c}") for c in range(len(stationary))]
+        for c, lhsT in enumerate(stationary):
+            nc.tensor.matmul(sums[c][:], lhsT, positions[:], start=True, stop=False)
+        for c, lhsT in enumerate(stationary):
+            nc.tensor.matmul(sums[c][:], lhsT, window[:].indirect(offsets[:]), start=False, stop=True)
+
+        for c in range(len(stationary)):
+            staged = held.tile([P, TOKENS], F32, name=f"staged{c}")
+            if c < Q_BLOCKS:
+                nc.vector.tensor_scalar_add(staged[:], sums[c][:], bias[:, c : c + 1])
+            else:
+                nc.vector.tensor_copy(staged[:], sums[c][:])
+            nc.sync.dma_start(out[c * P : (c + 1) * P, :], staged[:])

@@ -12,6 +12,9 @@ WORD_BLOCKS = WORDS // P
 
 FLOPS = 2 * P * Q * TOKENS
 
+WARM_COLUMNS = 512
+WARM_MATMULS = 5
+
 
 def tile_transformertranducer_kernel(tc, table, pos, w, b, offs, out):
     nc = tc.nc
@@ -19,6 +22,12 @@ def tile_transformertranducer_kernel(tc, table, pos, w, b, offs, out):
         tc.tile_pool(name="held", bufs=1) as held,
         tc.psum_pool(name="psum", bufs=1) as psum,
     ):
+        zeros = held.tile([P, WARM_COLUMNS], BF16, name="zeros")
+        nc.vector.memset(zeros[:], 0.0)
+        unread = psum.tile([P, WARM_COLUMNS], F32, name="unread")
+        for repeat in range(WARM_MATMULS):
+            nc.tensor.matmul(unread[:], zeros[:, 0:P], zeros[:], start=True, stop=True)
+
         word_rows = [held.tile([P, P], BF16, name=f"word_rows{h}") for h in range(WORD_BLOCKS)]
         nc.sync.dma_start(word_rows[0][:], table[0:P, :])
         nc.scalar.dma_start(word_rows[1][:], table[P : 2 * P, :])

@@ -2,6 +2,8 @@ import concourse.mybir as mybir
 from concourse.masks import make_identity
 
 BF16, F32, U16 = mybir.dt.bfloat16, mybir.dt.float32, mybir.dt.uint16
+ADD = mybir.AluOpType.add
+IDENTITY = mybir.ActivationFunctionType.Identity
 
 P = 128
 WORDS = 256
@@ -12,9 +14,6 @@ WORD_BLOCKS = WORDS // P
 
 FLOPS = 2 * P * Q * TOKENS
 
-WARM_COLUMNS = 512
-WARM_MATMULS = 5
-
 
 def tile_transformertranducer_kernel(tc, table, pos, w, b, offs, out):
     nc = tc.nc
@@ -22,12 +21,6 @@ def tile_transformertranducer_kernel(tc, table, pos, w, b, offs, out):
         tc.tile_pool(name="held", bufs=1) as held,
         tc.psum_pool(name="psum", bufs=1) as psum,
     ):
-        zeros = held.tile([P, WARM_COLUMNS], BF16, name="zeros")
-        nc.vector.memset(zeros[:], 0.0)
-        unread = psum.tile([P, WARM_COLUMNS], F32, name="unread")
-        for repeat in range(WARM_MATMULS):
-            nc.tensor.matmul(unread[:], zeros[:, 0:P], zeros[:], start=True, stop=True)
-
         word_rows = [held.tile([P, P], BF16, name=f"word_rows{h}") for h in range(WORD_BLOCKS)]
         nc.sync.dma_start(word_rows[0][:], table[0:P, :])
         nc.scalar.dma_start(word_rows[1][:], table[P : 2 * P, :])
@@ -50,17 +43,30 @@ def tile_transformertranducer_kernel(tc, table, pos, w, b, offs, out):
             nc.tensor.transpose(flipped[:], word_rows[h][:], identity[:])
             nc.vector.tensor_copy(window[:, h * P : (h + 1) * P], flipped[:])
 
-        stationary = [weights[:, c * P : (c + 1) * P] for c in range(Q_BLOCKS)] + [identity[:]]
-        sums = [psum.tile([P, TOKENS], F32, name=f"sums{c}") for c in range(len(stationary))]
-        for c, lhsT in enumerate(stationary):
-            nc.tensor.matmul(sums[c][:], lhsT, positions[:], start=True, stop=False)
-        for c, lhsT in enumerate(stationary):
-            nc.tensor.matmul(sums[c][:], lhsT, window[:].indirect(offsets[:]), start=False, stop=True)
+        projected = [psum.tile([P, TOKENS], F32, name=f"projected{c}") for c in range(Q_BLOCKS)]
+        for c in range(Q_BLOCKS):
+            nc.tensor.matmul(
+                projected[c][:], weights[:, c * P : (c + 1) * P], positions[:], start=True, stop=False
+            )
 
-        for c in range(len(stationary)):
-            staged = held.tile([P, TOKENS], F32, name=f"staged{c}")
-            if c < Q_BLOCKS:
-                nc.vector.tensor_scalar_add(staged[:], sums[c][:], bias[:, c : c + 1])
+        words = psum.tile([P, TOKENS], F32, name="words")
+        nc.tensor.matmul(words[:], identity[:], window[:].indirect(offsets[:]), start=True, stop=True)
+        embedded = held.tile([P, TOKENS], F32, name="embedded")
+        nc.vector.tensor_tensor(embedded[:], words[:], positions[:], ADD)
+        nc.sync.dma_start(out[Q : Q + P, :], embedded[:])
+
+        for c in range(Q_BLOCKS):
+            nc.tensor.matmul(
+                projected[c][:],
+                weights[:, c * P : (c + 1) * P],
+                window[:].indirect(offsets[:]),
+                start=False,
+                stop=True,
+            )
+            biased = held.tile([P, TOKENS], F32, name=f"biased{c}")
+            if c % 2 == 0:
+                nc.scalar.activation(biased[:], projected[c][:], IDENTITY, bias=bias[:, c : c + 1])
+                nc.scalar.dma_start(out[c * P : (c + 1) * P, :], biased[:])
             else:
-                nc.vector.tensor_copy(staged[:], sums[c][:])
-            nc.sync.dma_start(out[c * P : (c + 1) * P, :], staged[:])
+                nc.vector.tensor_scalar_add(biased[:], projected[c][:], bias[:, c : c + 1])
+                nc.sync.dma_start(out[c * P : (c + 1) * P, :], biased[:])

@@ -3,7 +3,6 @@ from concourse.masks import make_identity
 
 BF16, F32, U16 = mybir.dt.bfloat16, mybir.dt.float32, mybir.dt.uint16
 ADD = mybir.AluOpType.add
-IDENTITY = mybir.ActivationFunctionType.Identity
 
 P = 128
 WORDS = 256
@@ -24,12 +23,12 @@ def tile_transformertranducer_kernel(tc, table, pos, w, b, offs, out):
         word_rows = [held.tile([P, P], BF16, name=f"word_rows{h}") for h in range(WORD_BLOCKS)]
         nc.sync.dma_start(word_rows[0][:], table[0:P, :])
         nc.scalar.dma_start(word_rows[1][:], table[P : 2 * P, :])
-        offsets = held.tile([P, TOKENS // 16], U16, name="offsets")
-        nc.sync.dma_start(offsets[:], offs)
         weights = held.tile([P, Q], BF16, name="weights")
         nc.scalar.dma_start(weights[:], w)
         positions = held.tile([P, TOKENS], BF16, name="positions")
         nc.sync.dma_start(positions[:], pos)
+        offsets = held.tile([P, TOKENS // 16], U16, name="offsets")
+        nc.sync.dma_start(offsets[:], offs)
         bias = held.tile([P, Q_BLOCKS], F32, name="bias")
         with nc.allow_non_contiguous_dma(reason="384 bias values, one to a partition and block"):
             nc.scalar.dma_start(bias[:], b.rearrange("(c p) one -> p (c one)", p=P))
@@ -64,9 +63,6 @@ def tile_transformertranducer_kernel(tc, table, pos, w, b, offs, out):
                 stop=True,
             )
             biased = held.tile([P, TOKENS], F32, name=f"biased{c}")
-            if c % 2 == 0:
-                nc.scalar.activation(biased[:], projected[c][:], IDENTITY, bias=bias[:, c : c + 1])
-                nc.scalar.dma_start(out[c * P : (c + 1) * P, :], biased[:])
-            else:
-                nc.vector.tensor_scalar_add(biased[:], projected[c][:], bias[:, c : c + 1])
-                nc.sync.dma_start(out[c * P : (c + 1) * P, :], biased[:])
+            nc.vector.tensor_scalar_add(biased[:], projected[c][:], bias[:, c : c + 1])
+            queue = nc.scalar if c % 2 == 0 else nc.sync
+            queue.dma_start(out[c * P : (c + 1) * P, :], biased[:])

@@ -64,5 +64,4 @@ def tile_transformertranducer_kernel(tc, table, pos, w, b, offs, out):
             )
             biased = held.tile([P, TOKENS], F32, name=f"biased{c}")
             nc.vector.tensor_scalar_add(biased[:], projected[c][:], bias[:, c : c + 1])
-            queue = nc.scalar if c % 2 == 0 else nc.sync
-            queue.dma_start(out[c * P : (c + 1) * P, :], biased[:])
+            nc.sync.dma_start(out[c * P : (c + 1) * P, :], biased[:])

@@ -22,16 +22,16 @@ def tile_transformertranducer_kernel(tc, table, pos, w, b, offs, out):
     ):
         word_rows = [held.tile([P, P], BF16, name=f"word_rows{h}") for h in range(WORD_BLOCKS)]
         nc.sync.dma_start(word_rows[0][:], table[0:P, :])
-        nc.scalar.dma_start(word_rows[1][:], table[P : 2 * P, :])
+        nc.sync.dma_start(word_rows[1][:], table[P : 2 * P, :])
         weights = held.tile([P, Q], BF16, name="weights")
-        nc.scalar.dma_start(weights[:], w)
+        nc.sync.dma_start(weights[:], w)
         positions = held.tile([P, TOKENS], BF16, name="positions")
         nc.sync.dma_start(positions[:], pos)
         offsets = held.tile([P, TOKENS // 16], U16, name="offsets")
         nc.sync.dma_start(offsets[:], offs)
         bias = held.tile([P, Q_BLOCKS], F32, name="bias")
         with nc.allow_non_contiguous_dma(reason="384 bias values, one to a partition and block"):
-            nc.scalar.dma_start(bias[:], b.rearrange("(c p) one -> p (c one)", p=P))
+            nc.sync.dma_start(bias[:], b.rearrange("(c p) one -> p (c one)", p=P))
 
         identity = held.tile([P, P], BF16, name="identity")
         make_identity(nc, identity[:])

@@ -36,11 +36,11 @@ def tile_transformertranducer_kernel(tc, table, pos, w, b, offs, out):
         identity = held.tile([P, P], BF16, name="identity")
         make_identity(nc, identity[:])
 
-        window = held.tile([P, WORDS], BF16, name="window")
+        flipped = psum.tile([P, WORDS], BF16, name="flipped")
         for h in range(WORD_BLOCKS):
-            flipped = psum.tile([P, P], BF16, name=f"flipped{h}")
-            nc.tensor.transpose(flipped[:], word_rows[h][:], identity[:])
-            nc.vector.tensor_copy(window[:, h * P : (h + 1) * P], flipped[:])
+            nc.tensor.transpose(flipped[:, h * P : (h + 1) * P], word_rows[h][:], identity[:])
+        window = held.tile([P, WORDS], BF16, name="window")
+        nc.vector.tensor_copy(window[:], flipped[:])
 
         projected = [psum.tile([P, TOKENS], F32, name=f"projected{c}") for c in range(Q_BLOCKS)]
         for c in range(Q_BLOCKS):

@@ -48,11 +48,12 @@ def tile_transformertranducer_kernel(tc, table, pos, w, b, offs, out):
                 projected[c][:], weights[:, c * P : (c + 1) * P], positions[:], start=True, stop=False
             )
 
+        results = held.tile([P, 1 + Q_BLOCKS, TOKENS], F32, name="results")
+
         words = psum.tile([P, TOKENS], F32, name="words")
         nc.tensor.matmul(words[:], identity[:], window[:].indirect(offsets[:]), start=True, stop=True)
-        embedded = held.tile([P, TOKENS], F32, name="embedded")
-        nc.vector.tensor_tensor(embedded[:], words[:], positions[:], ADD)
-        nc.sync.dma_start(out[Q : Q + P, :], embedded[:])
+        nc.vector.tensor_tensor(results[:, 0, :], words[:], positions[:], ADD)
+        nc.sync.dma_start(out[Q : Q + P, :], results[:, 0, :])
 
         for c in range(Q_BLOCKS):
             nc.tensor.matmul(
@@ -62,6 +63,7 @@ def tile_transformertranducer_kernel(tc, table, pos, w, b, offs, out):
                 start=False,
                 stop=True,
             )
-            biased = held.tile([P, TOKENS], F32, name=f"biased{c}")
-            nc.vector.tensor_scalar_add(biased[:], projected[c][:], bias[:, c : c + 1])
-            nc.sync.dma_start(out[c * P : (c + 1) * P, :], biased[:])
+            nc.vector.tensor_scalar_add(results[:, 1 + c, :], projected[c][:], bias[:, c : c + 1])
+        nc.sync.dma_start(
+            out[0:Q, :].rearrange("(c p) j -> p c j", p=P), results[:, 1 : 1 + Q_BLOCKS, :]
+        )

@@ -25,8 +25,9 @@ def tile_transformertranducer_kernel(tc, table, pos, w, b, offs, out):
         nc.sync.dma_start(word_rows[1][:], table[P : 2 * P, :])
         weights = held.tile([P, Q], BF16, name="weights")
         nc.sync.dma_start(weights[:], w)
-        positions = held.tile([P, TOKENS], BF16, name="positions")
-        nc.sync.dma_start(positions[:], pos)
+        run = TOKENS + 2
+        positions = held.tile([P, run], BF16, name="positions")
+        nc.sync.dma_start(positions[:, :TOKENS], pos)
         offsets = held.tile([P, TOKENS // 16], U16, name="offsets")
         nc.sync.dma_start(offsets[:], offs)
         bias = held.tile([P, Q_BLOCKS], F32, name="bias")
@@ -35,6 +36,7 @@ def tile_transformertranducer_kernel(tc, table, pos, w, b, offs, out):
 
         identity = held.tile([P, P], BF16, name="identity")
         make_identity(nc, identity[:])
+        nc.gpsimd.tensor_copy(positions[:, TOKENS:], identity[:, : run - TOKENS])
 
         flipped = psum.tile([P, WORDS], BF16, name="flipped")
         for h in range(WORD_BLOCKS):
@@ -42,7 +44,7 @@ def tile_transformertranducer_kernel(tc, table, pos, w, b, offs, out):
         window = held.tile([P, WORDS], BF16, name="window")
         nc.vector.tensor_copy(window[:], flipped[:])
 
-        projected = [psum.tile([P, TOKENS], F32, name=f"projected{c}") for c in range(Q_BLOCKS)]
+        projected = [psum.tile([P, run], F32, name=f"projected{c}") for c in range(Q_BLOCKS)]
         for c in range(Q_BLOCKS):
             nc.tensor.matmul(
                 projected[c][:], weights[:, c * P : (c + 1) * P], positions[:], start=True, stop=False
@@ -52,18 +54,18 @@ def tile_transformertranducer_kernel(tc, table, pos, w, b, offs, out):
 
         words = psum.tile([P, TOKENS], F32, name="words")
         nc.tensor.matmul(words[:], identity[:], window[:].indirect(offsets[:]), start=True, stop=True)
-        nc.vector.tensor_tensor(results[:, 0, :], words[:], positions[:], ADD)
+        nc.vector.tensor_tensor(results[:, 0, :], words[:], positions[:, :TOKENS], ADD)
         nc.sync.dma_start(out[Q : Q + P, :], results[:, 0, :])
 
         for c in range(Q_BLOCKS):
             nc.tensor.matmul(
-                projected[c][:],
+                projected[c][:, :TOKENS],
                 weights[:, c * P : (c + 1) * P],
                 window[:].indirect(offsets[:]),
                 start=False,
                 stop=True,
             )
-            nc.vector.tensor_scalar_add(results[:, 1 + c, :], projected[c][:], bias[:, c : c + 1])
+            nc.vector.tensor_scalar_add(results[:, 1 + c, :], projected[c][:, :TOKENS], bias[:, c : c + 1])
         nc.sync.dma_start(
             out[0:Q, :].rearrange("(c p) j -> p c j", p=P), results[:, 1 : 1 + Q_BLOCKS, :]
         )

@@ -38,11 +38,11 @@ def tile_transformertranducer_kernel(tc, table, pos, w, b, offs, out):
         make_identity(nc, identity[:])
         nc.gpsimd.tensor_copy(positions[:, TOKENS:], identity[:, : run - TOKENS])
 
-        flipped = psum.tile([P, WORDS], BF16, name="flipped")
-        for h in range(WORD_BLOCKS):
-            nc.tensor.transpose(flipped[:, h * P : (h + 1) * P], word_rows[h][:], identity[:])
         window = held.tile([P, WORDS], BF16, name="window")
-        nc.vector.tensor_copy(window[:], flipped[:])
+        for h in range(WORD_BLOCKS):
+            flipped = psum.tile([P, P], BF16, name=f"flipped{h}")
+            nc.tensor.transpose(flipped[:], word_rows[h][:], identity[:])
+            nc.vector.tensor_copy(window[:, h * P : (h + 1) * P], flipped[:])
 
         projected = [psum.tile([P, run], F32, name=f"projected{c}") for c in range(Q_BLOCKS)]
         for c in range(Q_BLOCKS):

@@ -31,8 +31,7 @@ def tile_transformertranducer_kernel(tc, table, pos, w, b, offs, out):
         offsets = held.tile([P, TOKENS // 16], U16, name="offsets")
         nc.sync.dma_start(offsets[:], offs)
         bias = held.tile([P, Q_BLOCKS], F32, name="bias")
-        with nc.allow_non_contiguous_dma(reason="384 bias values, one to a partition and block"):
-            nc.sync.dma_start(bias[:], b.rearrange("(c p) one -> p (c one)", p=P))
+        nc.sync.dma_start(bias[:], b.rearrange("(p c) one -> p (c one)", c=Q_BLOCKS))
 
         identity = held.tile([P, P], BF16, name="identity")
         make_identity(nc, identity[:])
@@ -44,10 +43,14 @@ def tile_transformertranducer_kernel(tc, table, pos, w, b, offs, out):
             nc.tensor.transpose(flipped[:], word_rows[h][:], identity[:])
             nc.vector.tensor_copy(window[:, h * P : (h + 1) * P], flipped[:])
 
+        dealt = [held.tile([P, P], BF16, name=f"dealt{c}") for c in range(Q_BLOCKS)]
+        for c in range(Q_BLOCKS):
+            nc.scalar.copy(dealt[c][:], weights[:, c::Q_BLOCKS])
+
         projected = [psum.tile([P, run], F32, name=f"projected{c}") for c in range(Q_BLOCKS)]
         for c in range(Q_BLOCKS):
             nc.tensor.matmul(
-                projected[c][:], weights[:, c * P : (c + 1) * P], positions[:], start=True, stop=False
+                projected[c][:], weights[:, c::Q_BLOCKS], positions[:], start=True, stop=False
             )
 
         results = held.tile([P, 1 + Q_BLOCKS, TOKENS], F32, name="results")
@@ -60,12 +63,12 @@ def tile_transformertranducer_kernel(tc, table, pos, w, b, offs, out):
         for c in range(Q_BLOCKS):
             nc.tensor.matmul(
                 projected[c][:, :TOKENS],
-                weights[:, c * P : (c + 1) * P],
+                dealt[c][:],
                 window[:].indirect(offsets[:]),
                 start=False,
                 stop=True,
             )
             nc.vector.tensor_scalar_add(results[:, 1 + c, :], projected[c][:, :TOKENS], bias[:, c : c + 1])
         nc.sync.dma_start(
-            out[0:Q, :].rearrange("(c p) j -> p c j", p=P), results[:, 1 : 1 + Q_BLOCKS, :]
+            out[0:Q, :].rearrange("(p c) j -> p c j", c=Q_BLOCKS), results[:, 1 : 1 + Q_BLOCKS, :]
         )

@@ -23,11 +23,11 @@ def tile_transformertranducer_kernel(tc, table, pos, w, b, offs, out):
         word_rows = [held.tile([P, P], BF16, name=f"word_rows{h}") for h in range(WORD_BLOCKS)]
         nc.sync.dma_start(word_rows[0][:], table[0:P, :])
         nc.sync.dma_start(word_rows[1][:], table[P : 2 * P, :])
-        weights = held.tile([P, Q], BF16, name="weights")
-        nc.sync.dma_start(weights[:], w)
         run = TOKENS + 2
         positions = held.tile([P, run], BF16, name="positions")
         nc.sync.dma_start(positions[:, :TOKENS], pos)
+        weights = held.tile([P, Q], BF16, name="weights")
+        nc.sync.dma_start(weights[:], w)
         offsets = held.tile([P, TOKENS // 16], U16, name="offsets")
         nc.sync.dma_start(offsets[:], offs)
         bias = held.tile([P, Q_BLOCKS], F32, name="bias")

@@ -34,7 +34,8 @@ def tile_transformertranducer_kernel(tc, table, pos, w, b, offs, out):
         nc.sync.dma_start(bias[:], b.rearrange("(p c) one -> p (c one)", c=Q_BLOCKS))
 
         identity = held.tile([P, P], BF16, name="identity")
-        make_identity(nc, identity[:])
+        nc.vector.memset(identity[:], 0.0)
+        make_identity(nc, identity[:], nomemset=True)
         nc.gpsimd.tensor_copy(positions[:, TOKENS:], identity[:, : run - TOKENS])
 
         window = held.tile([P, WORDS], BF16, name="window")

import concourse.mybir as mybir
from concourse.masks import make_identity

BF16, F32, U16 = mybir.dt.bfloat16, mybir.dt.float32, mybir.dt.uint16
ADD = mybir.AluOpType.add

P = 128
WORDS = 256
TOKENS = 128
Q = 384
Q_BLOCKS = Q // P
WORD_BLOCKS = WORDS // P

FLOPS = 2 * P * Q * TOKENS


def tile_transformertranducer_kernel(tc, table, pos, w, b, offs, out):
    nc = tc.nc
    with (
        tc.tile_pool(name="held", bufs=1) as held,
        tc.psum_pool(name="psum", bufs=1) as psum,
    ):
        word_rows = [held.tile([P, P], BF16, name=f"word_rows{h}") for h in range(WORD_BLOCKS)]
        nc.sync.dma_start(word_rows[0][:], table[0:P, :])
        nc.sync.dma_start(word_rows[1][:], table[P : 2 * P, :])
        run = TOKENS + 2
        positions = held.tile([P, run], BF16, name="positions")
        nc.sync.dma_start(positions[:, :TOKENS], pos)
        weights = held.tile([P, Q], BF16, name="weights")
        nc.sync.dma_start(weights[:], w)
        offsets = held.tile([P, TOKENS // 16], U16, name="offsets")
        nc.sync.dma_start(offsets[:], offs)
        bias = held.tile([P, Q_BLOCKS], F32, name="bias")
        nc.sync.dma_start(bias[:], b.rearrange("(p c) one -> p (c one)", c=Q_BLOCKS))

        identity = held.tile([P, P], BF16, name="identity")
        nc.vector.memset(identity[:], 0.0)
        make_identity(nc, identity[:], nomemset=True)
        nc.gpsimd.tensor_copy(positions[:, TOKENS:], identity[:, : run - TOKENS])

        window = held.tile([P, WORDS], BF16, name="window")
        for h in range(WORD_BLOCKS):
            flipped = psum.tile([P, P], BF16, name=f"flipped{h}")
            nc.tensor.transpose(flipped[:], word_rows[h][:], identity[:])
            nc.vector.tensor_copy(window[:, h * P : (h + 1) * P], flipped[:])

        dealt = [held.tile([P, P], BF16, name=f"dealt{c}") for c in range(Q_BLOCKS)]
        for c in range(Q_BLOCKS):
            nc.scalar.copy(dealt[c][:], weights[:, c::Q_BLOCKS])

        projected = [psum.tile([P, run], F32, name=f"projected{c}") for c in range(Q_BLOCKS)]
        for c in range(Q_BLOCKS):
            nc.tensor.matmul(
                projected[c][:], weights[:, c::Q_BLOCKS], positions[:], start=True, stop=False
            )

        results = held.tile([P, 1 + Q_BLOCKS, TOKENS], F32, name="results")

        words = psum.tile([P, TOKENS], F32, name="words")
        nc.tensor.matmul(words[:], identity[:], window[:].indirect(offsets[:]), start=True, stop=True)
        nc.vector.tensor_tensor(results[:, 0, :], words[:], positions[:, :TOKENS], ADD)
        nc.sync.dma_start(out[Q : Q + P, :], results[:, 0, :])

        for c in range(Q_BLOCKS):
            nc.tensor.matmul(
                projected[c][:, :TOKENS],
                dealt[c][:],
                window[:].indirect(offsets[:]),
                start=False,
                stop=True,
            )
            nc.vector.tensor_scalar_add(results[:, 1 + c, :], projected[c][:, :TOKENS], bias[:, c : c + 1])
        nc.sync.dma_start(
            out[0:Q, :].rearrange("(p c) j -> p c j", c=Q_BLOCKS), results[:, 1 : 1 + Q_BLOCKS, :]
        )
